import numpy as np
import ml_dtypes


def mxq(x, axis, fmt="e4m3"):
    dtype, down = {"e4m3": (ml_dtypes.float8_e4m3fn, 7), "e5m2": (ml_dtypes.float8_e5m2, 14)}[fmt]
    v = np.moveaxis(np.asarray(x, np.float32).astype(ml_dtypes.bfloat16).astype(np.float64), axis, -1)
    blocks = v.reshape(v.shape[:-1] + (-1, 32))
    amax = np.abs(blocks).max(-1, keepdims=True)
    byte = np.maximum(np.where(amax > 0, np.frexp(amax)[1] - 1 + 127, 0) - down, 1)
    scale = np.exp2(byte - 127.0)
    codes = (blocks / scale).astype(np.float32).astype(dtype).astype(np.float64)
    return np.moveaxis((codes * scale).reshape(v.shape), -1, axis)


WIDE = False


def mx_kscale(k):
    if not WIDE:
        return np.ones(k)
    levels = np.array([10, -10, 5, -5, 0])
    a = np.random.permutation(np.resize(levels, k // 512 * 4)).reshape(k // 512, 4)
    idx = np.arange(k)
    return np.exp2(a[idx // 512, idx % 128 // 32])


BF16 = ml_dtypes.bfloat16


def bf(x):
    return np.asarray(x, np.float32).astype(BF16)


def f64(x):
    return np.asarray(x).astype(np.float64)


B, C, H, D, N, CO = 4, 128, 2048, 512, 4, 512
NC = N * C
EPS = 1e-5


def bn(v, gamma, beta, axes):
    mean = v.mean(axis=axes, keepdims=True)
    var = v.var(axis=axes, keepdims=True)
    return (v - mean) / np.sqrt(var + EPS) * gamma + beta


def setup_inputs():
    u = mx_kscale(NC)
    head = np.maximum(np.random.standard_normal((N, B, C, D)), 0.0) + 0.25 * np.random.standard_normal((N, B, C, D))
    return {'head_res': bf(head * u.reshape(N, 1, C, 1)),
            'W_merge': bf(np.random.standard_normal((CO, NC)) / np.sqrt(NC) / u[None, :]),
            'g_m': bf(1.0 + 0.1 * np.random.standard_normal(CO)),
            'b_m': bf(0.1 * np.random.standard_normal(CO))}


def reference(head_res, W_merge, g_m, b_m):
    cat = f64(head_res).transpose(1, 0, 2, 3).reshape(B, NC, D)
    m = mxq(f64(W_merge), 1, 'e4m3')[None] @ mxq(cat, 1, 'e4m3')
    m = bn(m, f64(g_m)[None, :, None], f64(b_m)[None, :, None], (0, 2))
    return np.maximum(m, 0.0)

@@ -1,0 +1,262 @@
+from contextlib import ExitStack
+
+import concourse.mybir as mybir
+from concourse.masks import make_identity
+
+FLOPS = 2 * 512 * 512 * 2048
+
+F32 = mybir.dt.float32
+BF16 = mybir.dt.bfloat16
+U32 = mybir.dt.uint32
+U8 = mybir.dt.uint8
+FP8X4 = mybir.dt.float8_e4m3fn_x4
+ACT = mybir.ActivationFunctionType
+ALU = mybir.AluOpType
+
+P = 128
+HEADS = 4
+BATCH = 4
+D = 512
+MT = 4
+EPS = 1e-5
+
+V_COLS = (352,288,224,256)
+V_APPLY = ()
+ORDER = {
+    "sync": [("ldw", 0), ("ldr", 0), ("ldr", 1), ("ldr", 2), ("ldr", 3), ("ldw", 1), ("so", 0, 0), ("so", 0, 1), ("so", 0, 2), ("so", 0, 3), ("so", 1, 0), ("so", 1, 1), ("so", 1, 2), ("so", 1, 3), ("so", 2, 0), ("so", 2, 1), ("so", 2, 2), ("so", 2, 3), ("so", 3, 0), ("so", 3, 2), ("so", 3, 1), ("so", 3, 3)],
+    "pe": [("tr", 0), ("tr", 1), ("mm", 0, 0), ("mm", 0, 1), ("tr", 2), ("tr", 3), ("mm", 0, 2), ("mm", 0, 3), ("mm", 1, 0), ("mm", 1, 1), ("mm", 1, 2), ("mm", 1, 3), ("mm", 2, 0), ("mm", 2, 1), ("mm", 2, 2), ("mm", 2, 3), ("mm", 3, 0), ("mm", 3, 1), ("mm", 3, 2), ("mm", 3, 3)],
+    "act": [("ldgb",), ("warm",), ("evacS", 0), ("rgS", 0), ("evacS", 1), ("rgS", 1), ("rgS", 2), ("rgS", 3), ("evacS", 2), ("evacS", 3), ("rstd", 0), ("stS", 0), ("ap", 0, 0), ("ap", 0, 1), ("ap", 0, 2), ("ap", 0, 3), ("rstd", 1), ("stS", 1), ("ap", 1, 0), ("ap", 1, 1), ("ap", 1, 2), ("rstd", 2), ("ap", 1, 3), ("ap", 2, 0), ("ap", 2, 1), ("ap", 2, 2), ("rstd", 3), ("ap", 2, 3), ("ap", 3, 0), ("ap", 3, 1)],
+    "dve": [("eps",), ("cast",), ("rgV", 0), ("q", 0), ("qw", 0, 2), ("rgV", 1), ("q", 1), ("st", 0, 0), ("rgV", 2), ("rgV", 3), ("q", 2), ("q", 3), ("st", 0, 1), ("st", 0, 2), ("st", 0, 3), ("ag", 0), ("qw", 2, 4), ("st", 1, 0), ("st", 1, 1), ("st", 1, 2), ("st", 1, 3), ("ag", 1), ("st", 2, 0), ("st", 2, 1), ("st", 2, 2), ("st", 2, 3), ("ag", 2), ("st", 3, 0), ("stV", 2), ("st", 3, 1), ("st", 3, 2), ("st", 3, 3), ("ag", 3), ("stV", 3), ("apV", 3, 2), ("rlV", 3, 2), ("apV", 3, 3), ("rlV", 3, 3)],
+    "pool": [("ident",)],
+}
+
+
+def tile_block_height_reducing_filtering_pb_kernel(tc, head_res, W_merge, g_m, b_m, out):
+    nc = tc.nc
+    with ExitStack() as ctx:
+        keep = ctx.enter_context(tc.tile_pool(name="keep", bufs=1))
+        psum = ctx.enter_context(tc.psum_pool(name="psum", bufs=1))
+        ctx.enter_context(tc.manual_schedule())
+
+        w_sb = keep.tile([P, MT, HEADS * P], BF16, name="w_sb")
+        raw = [keep.tile([P, HEADS, D], BF16, name="raw%d" % b) for b in range(BATCH)]
+        grouped = [keep.tile([P, D, HEADS], BF16, name="grouped%d" % b, align_bytes=64) for b in range(BATCH)]
+        g16 = keep.tile([P, MT], BF16, name="g16")
+        b16 = keep.tile([P, MT], BF16, name="b16")
+        g32 = keep.tile([P, MT], F32, name="g32")
+        b32 = keep.tile([P, MT], F32, name="b32")
+        ident = keep.tile([P, P], BF16, name="ident")
+        eps = keep.tile([P, 1], F32, name="eps")
+        warm = keep.tile([P, 1], F32, name="warm")
+        gw = keep.tile([P, MT, P, HEADS], BF16, name="gw", align_bytes=64)
+        w_codes = keep.tile([P, MT, P], U32, name="w_codes", align_bytes=64)
+        w_scl = keep.tile([P, MT, P], U8, name="w_scl", align_bytes=64)
+        c_codes = keep.tile([P, BATCH, D], U32, name="c_codes", align_bytes=64)
+        c_scl = keep.tile([P, BATCH, D], U8, name="c_scl", align_bytes=64)
+        stats = [keep.tile([P, BATCH, 6], F32, name="stats%d" % m) for m in range(MT)]
+        mv = [keep.tile([P, 2], F32, name="mv%d" % m) for m in range(MT)]
+        gm = [keep.tile([P, 1], F32, name="gm%d" % m) for m in range(MT)]
+        rstd = [keep.tile([P, 1], F32, name="rstd%d" % m) for m in range(MT)]
+        s_col = [keep.tile([P, 1], F32, name="s_col%d" % m) for m in range(MT)]
+        t_col = [keep.tile([P, 1], F32, name="t_col%d" % m) for m in range(MT)]
+        o_sb = [keep.tile([P, BATCH, D], F32, name="o_sb%d" % m) for m in range(MT)]
+        wt = {}
+        acc = {}
+        w_view = W_merge.rearrange("(p m) k -> p m k", m=MT)
+        out_v = out.rearrange("b (p m) d -> m p b d", m=MT)
+
+        def regroup(copy, b, c0, c1):
+            copy(
+                out=grouped[b][:, c0:c1, :].rearrange("p (c i) t -> p c t i", i=4),
+                in_=raw[b][:, :, c0:c1].rearrange("p t (c i) -> p c t i", i=4),
+            )
+
+        def run(op):
+            kind = op[0]
+            if kind == "ldw":
+                h = op[1]
+                nc.sync.dma_start(out=w_sb[:, 2 * h:2 * h + 2, :], in_=w_view[:, 2 * h:2 * h + 2, :])
+            elif kind == "ldr":
+                b = op[1]
+                nc.sync.dma_start(out=raw[b][:], in_=head_res[:, b].rearrange("n c d -> c n d"))
+            elif kind == "ldgb":
+                nc.scalar.dma_start(out=g16[:], in_=g_m.rearrange("(p m) -> p m", m=MT))
+                nc.scalar.dma_start(out=b16[:], in_=b_m.rearrange("(p m) -> p m", m=MT))
+            elif kind == "ident":
+                make_identity(nc, ident[:])
+            elif kind == "eps":
+                nc.vector.memset(eps[:], EPS)
+            elif kind == "warm":
+                nc.scalar.activation(out=warm[:], in_=eps[:], func=ACT.Abs_reciprocal_sqrt)
+            elif kind == "cast":
+                nc.vector.tensor_copy(out=g32[:], in_=g16[:])
+                nc.vector.tensor_copy(out=b32[:], in_=b16[:])
+            elif kind == "tr":
+                m = op[1]
+                wt[m] = psum.tile([P, HEADS, P], BF16, name="wt%d" % m, tag="bank%d" % (4 + m))
+                for t in range(HEADS):
+                    nc.tensor.transpose(wt[m][:, t, :], w_sb[:, m, t * P:(t + 1) * P], ident[:])
+            elif kind == "evacS" or kind == "evacV":
+                m = op[1]
+                copy = nc.scalar.copy if kind == "evacS" else nc.vector.tensor_copy
+                copy(out=gw[:, m, :, :], in_=wt[m][:].rearrange("p t o -> p o t"))
+            elif kind == "qw":
+                m0, m1 = op[1], op[2]
+                nc.vector.quantize_mx(
+                    out=w_codes[:, m0:m1, :].rearrange("p m o -> p (m o)").bitcast(FP8X4),
+                    scales=w_scl[:, m0:m1, :].rearrange("p m o -> p (m o)"),
+                    in_=gw[:, m0:m1, :, :].rearrange("p m o t -> p (m o t)"),
+                )
+            elif kind == "rgV":
+                regroup(nc.vector.tensor_copy, op[1], 0, V_COLS[op[1]])
+            elif kind == "rgS":
+                regroup(nc.scalar.copy, op[1], V_COLS[op[1]], D)
+            elif kind == "q":
+                b = op[1]
+                nc.vector.quantize_mx(
+                    out=c_codes[:, b, :].bitcast(FP8X4),
+                    scales=c_scl[:, b, :],
+                    in_=grouped[b][:].rearrange("p w j -> p (w j)"),
+                )
+            elif kind == "mm":
+                m, b = op[1], op[2]
+                acc[(m, b)] = psum.tile([P, D], F32, name="acc%d_%d" % (m, b), tag="bank%d" % (4 * (m % 2) + b))
+                nc.tensor.matmul_mx(
+                    out=acc[(m, b)][:],
+                    lhsT=w_codes[:, m, :].bitcast(FP8X4),
+                    lhsT_scale=w_scl[:, m, :],
+                    rhs=c_codes[:, b, :].bitcast(FP8X4),
+                    rhs_scale=c_scl[:, b, :],
+                    start=True,
+                    stop=True,
+                )
+            elif kind == "st":
+                m, b = op[1], op[2]
+                nc.vector.bn_stats(out=stats[m][:, b, :], in_=acc[(m, b)][:])
+            elif kind == "ag":
+                m = op[1]
+                nc.vector.bn_aggr(out=mv[m][:], in_=stats[m][:].rearrange("p b s -> p (b s)"))
+                nc.vector.scalar_tensor_tensor(
+                    out=gm[m][:], in0=mv[m][:, 0:1], scalar=-1.0, in1=g32[:, m:m + 1], op0=ALU.mult, op1=ALU.mult
+                )
+            elif kind == "rstd":
+                m = op[1]
+                nc.scalar.activation(
+                    out=rstd[m][:], in_=mv[m][:, 1:2], func=ACT.Abs_reciprocal_sqrt, bias=eps[:, 0:1]
+                )
+            elif kind == "stS":
+                m = op[1]
+                nc.scalar.activation(out=s_col[m][:], in_=g32[:, m:m + 1], func=ACT.Copy, scale=rstd[m][:, 0:1])
+                nc.scalar.activation(
+                    out=t_col[m][:], in_=gm[m][:], func=ACT.Identity, scale=rstd[m][:, 0:1], bias=b32[:, m:m + 1]
+                )
+            elif kind == "stV":
+                m = op[1]
+                nc.vector.tensor_mul(out=s_col[m][:], in0=g32[:, m:m + 1], in1=rstd[m][:])
+                nc.vector.scalar_tensor_tensor(
+                    out=t_col[m][:], in0=gm[m][:], scalar=rstd[m][:, 0:1], in1=b32[:, m:m + 1],
+                    op0=ALU.mult, op1=ALU.add,
+                )
+            elif kind == "ap":
+                m, b = op[1], op[2]
+                nc.scalar.activation(
+                    out=o_sb[m][:, b, :], in_=acc[(m, b)][:], func=ACT.Relu,
+                    scale=s_col[m][:, 0:1], bias=t_col[m][:, 0:1],
+                )
+            elif kind == "apV":
+                m, b = op[1], op[2]
+                nc.vector.tensor_scalar(
+                    out=o_sb[m][:, b, :], in0=acc[(m, b)][:], scalar1=s_col[m][:, 0:1], scalar2=t_col[m][:, 0:1],
+                    op0=ALU.mult, op1=ALU.add,
+                )
+            elif kind == "rlV":
+                m, b = op[1], op[2]
+                nc.vector.tensor_scalar_max(out=o_sb[m][:, b, :], in0=o_sb[m][:, b, :], scalar1=0.0)
+            elif kind == "rlG":
+                m, b = op[1], op[2]
+                nc.gpsimd.tensor_scalar(
+                    out=o_sb[m][:, b, :], in0=o_sb[m][:, b, :], scalar1=0.0, scalar2=0.0, op0=ALU.max, op1=ALU.add
+                )
+            elif kind == "so":
+                m, b = op[1], op[2]
+                nc.sync.dma_start(out=out_v[m][:, b, :], in_=o_sb[m][:, b, :])
+            else:
+                raise ValueError(kind)
+
+        def needs(op):
+            kind = op[0]
+            if kind == "warm":
+                return [("eps",)]
+            if kind == "cast":
+                return [("ldgb",)]
+            if kind == "tr":
+                return [("ldw", op[1] // 2), ("ident",)]
+            if kind == "evacS" or kind == "evacV":
+                return [("tr", op[1])]
+            if kind == "qw":
+                return [("evac", m) for m in range(op[1], op[2])]
+            if kind == "rgV" or kind == "rgS":
+                return [("ldr", op[1])]
+            if kind == "q":
+                return [("rgV", op[1]), ("rgS", op[1])]
+            if kind == "mm":
+                m, b = op[1], op[2]
+                first = [("qwm", m), ("q", b)]
+                if m == 1:
+                    first.append(("evac", b))
+                if m >= 2:
+                    first.append(("applied", m - 2, b))
+                return first
+            if kind == "st":
+                return [("mm", op[1], op[2])]
+            if kind == "ag":
+                return [("st", op[1], b) for b in range(BATCH)] + [("cast",)]
+            if kind == "rstd":
+                return [("ag", op[1]), ("eps",)]
+            if kind == "stS" or kind == "stV":
+                return [("rstd", op[1])]
+            if kind == "ap" or kind == "apV":
+                return [("scale", op[1]), ("st", op[1], op[2])]
+            if kind == "rlV" or kind == "rlG":
+                return [("apV", op[1], op[2])]
+            if kind == "so":
+                return [("ready", op[1], op[2])]
+            return []
+
+        def gives(op):
+            kind = op[0]
+            made = [op]
+            if kind == "evacS" or kind == "evacV":
+                made.append(("evac", op[1]))
+            if kind == "qw":
+                made.extend([("qwm", m) for m in range(op[1], op[2])])
+            if kind == "stS" or kind == "stV":
+                made.append(("scale", op[1]))
+            if kind == "ap":
+                made.extend([("applied", op[1], op[2]), ("ready", op[1], op[2])])
+            if kind == "apV":
+                made.append(("applied", op[1], op[2]))
+            if kind == "rlV" or kind == "rlG":
+                made.append(("ready", op[1], op[2]))
+            return made
+
+        done = set()
+        for b in range(BATCH):
+            if V_COLS[b] == 0:
+                done.add(("rgV", b))
+            if V_COLS[b] == D:
+                done.add(("rgS", b))
+        pos = dict((e, 0) for e in ORDER)
+        left = sum(len(ORDER[e]) for e in ORDER)
+        while left > 0:
+            moved = False
+            for e in ("sync", "pool", "pe", "dve", "act"):
+                while pos[e] < len(ORDER[e]) and all(n in done for n in needs(ORDER[e][pos[e]])):
+                    op = ORDER[e][pos[e]]
+                    run(op)
+                    for k in gives(op):
+                        done.add(k)
+                    pos[e] += 1
+                    left -= 1
+                    moved = True
+            assert moved, "the engines' orders wait for each other"

@@ -24,9 +24,9 @@ V_COLS = (352,288,224,256)
 V_APPLY = ()
 ORDER = {
     "sync": [("ldw", 0), ("ldr", 0), ("ldr", 1), ("ldr", 2), ("ldr", 3), ("ldw", 1), ("so", 0, 0), ("so", 0, 1), ("so", 0, 2), ("so", 0, 3), ("so", 1, 0), ("so", 1, 1), ("so", 1, 2), ("so", 1, 3), ("so", 2, 0), ("so", 2, 1), ("so", 2, 2), ("so", 2, 3), ("so", 3, 0), ("so", 3, 2), ("so", 3, 1), ("so", 3, 3)],
-    "pe": [("tr", 0), ("tr", 1), ("mm", 0, 0), ("mm", 0, 1), ("tr", 2), ("tr", 3), ("mm", 0, 2), ("mm", 0, 3), ("mm", 1, 0), ("mm", 1, 1), ("mm", 1, 2), ("mm", 1, 3), ("mm", 2, 0), ("mm", 2, 1), ("mm", 2, 2), ("mm", 2, 3), ("mm", 3, 0), ("mm", 3, 1), ("mm", 3, 2), ("mm", 3, 3)],
-    "act": [("ldgb",), ("warm",), ("evacS", 0), ("rgS", 0), ("evacS", 1), ("rgS", 1), ("rgS", 2), ("rgS", 3), ("evacS", 2), ("evacS", 3), ("rstd", 0), ("stS", 0), ("ap", 0, 0), ("ap", 0, 1), ("ap", 0, 2), ("ap", 0, 3), ("rstd", 1), ("stS", 1), ("ap", 1, 0), ("ap", 1, 1), ("ap", 1, 2), ("rstd", 2), ("ap", 1, 3), ("ap", 2, 0), ("ap", 2, 1), ("ap", 2, 2), ("rstd", 3), ("ap", 2, 3), ("ap", 3, 0), ("ap", 3, 1)],
-    "dve": [("eps",), ("cast",), ("rgV", 0), ("q", 0), ("qw", 0, 2), ("rgV", 1), ("q", 1), ("st", 0, 0), ("rgV", 2), ("rgV", 3), ("q", 2), ("q", 3), ("st", 0, 1), ("st", 0, 2), ("st", 0, 3), ("ag", 0), ("qw", 2, 4), ("st", 1, 0), ("st", 1, 1), ("st", 1, 2), ("st", 1, 3), ("ag", 1), ("st", 2, 0), ("st", 2, 1), ("st", 2, 2), ("st", 2, 3), ("ag", 2), ("st", 3, 0), ("stV", 2), ("st", 3, 1), ("st", 3, 2), ("st", 3, 3), ("ag", 3), ("stV", 3), ("apV", 3, 2), ("rlV", 3, 2), ("apV", 3, 3), ("rlV", 3, 3)],
+    "pe": [("tr", 0), ("tr", 1), ("mm", 0, 0), ("mm", 1, 0), ("mm", 0, 1), ("mm", 1, 1), ("tr", 2), ("tr", 3), ("mm", 0, 2), ("mm", 0, 3), ("mm", 1, 2), ("mm", 1, 3), ("mm", 2, 0), ("mm", 2, 1), ("mm", 2, 2), ("mm", 2, 3), ("mm", 3, 0), ("mm", 3, 1), ("mm", 3, 2), ("mm", 3, 3)],
+    "act": [("warm",), ("evacS", 0), ("rgS", 0), ("evacS", 1), ("ldgb",), ("rgS", 1), ("rgS", 2), ("rgS", 3), ("evacS", 2), ("evacS", 3), ("rstd", 0), ("stS", 0), ("ap", 0, 0), ("ap", 0, 1), ("ap", 0, 2), ("ap", 0, 3), ("rstd", 1), ("stS", 1), ("ap", 1, 0), ("ap", 1, 1), ("ap", 1, 2), ("rstd", 2), ("ap", 1, 3), ("ap", 2, 0), ("ap", 2, 1), ("ap", 2, 2), ("rstd", 3), ("ap", 2, 3), ("ap", 3, 0), ("ap", 3, 1)],
+    "dve": [("eps",), ("rgV", 0), ("q", 0), ("qw", 0, 2), ("rgV", 1), ("q", 1), ("st", 0, 0), ("rgV", 2), ("rgV", 3), ("q", 2), ("q", 3), ("cast",), ("st", 0, 1), ("st", 0, 2), ("st", 0, 3), ("ag", 0), ("qw", 2, 4), ("st", 1, 0), ("st", 1, 1), ("st", 1, 2), ("st", 1, 3), ("ag", 1), ("st", 2, 0), ("st", 2, 1), ("st", 2, 2), ("st", 2, 3), ("ag", 2), ("st", 3, 0), ("stV", 2), ("st", 3, 1), ("st", 3, 2), ("st", 3, 3), ("ag", 3), ("stV", 3), ("apV", 3, 2), ("rlV", 3, 2), ("apV", 3, 3), ("rlV", 3, 3)],
     "pool": [("ident",)],
 }
 

@@ -23,10 +23,10 @@ EPS = 1e-5
 V_COLS = (352,288,224,256)
 V_APPLY = ()
 ORDER = {
-    "sync": [("ldw", 0), ("ldr", 0), ("ldr", 1), ("ldr", 2), ("ldr", 3), ("ldw", 1), ("so", 0, 0), ("so", 0, 1), ("so", 0, 2), ("so", 0, 3), ("so", 1, 0), ("so", 1, 1), ("so", 1, 2), ("so", 1, 3), ("so", 2, 0), ("so", 2, 1), ("so", 2, 2), ("so", 2, 3), ("so", 3, 0), ("so", 3, 2), ("so", 3, 1), ("so", 3, 3)],
+    "sync": [("ldw", 0), ("ldr", 0), ("ldr", 1), ("ldr", 2), ("ldr", 3), ("ldw", 1), ("so", 0, 0), ("so", 0, 1), ("so", 0, 2), ("so", 0, 3), ("so", 1, 0), ("so", 1, 1), ("so", 1, 2), ("so", 1, 3), ("so", 2, 0), ("so", 2, 1), ("so", 2, 2), ("so", 2, 3), ("so", 3, 0), ("so", 3, 1), ("so", 3, 3), ("so", 3, 2)],
     "pe": [("tr", 0), ("tr", 1), ("mm", 0, 0), ("mm", 1, 0), ("mm", 0, 1), ("mm", 1, 1), ("tr", 2), ("tr", 3), ("mm", 0, 2), ("mm", 0, 3), ("mm", 1, 2), ("mm", 1, 3), ("mm", 2, 0), ("mm", 2, 1), ("mm", 2, 2), ("mm", 2, 3), ("mm", 3, 0), ("mm", 3, 1), ("mm", 3, 2), ("mm", 3, 3)],
-    "act": [("warm",), ("evacS", 0), ("rgS", 0), ("evacS", 1), ("ldgb",), ("rgS", 1), ("rgS", 2), ("rgS", 3), ("evacS", 2), ("evacS", 3), ("rstd", 0), ("stS", 0), ("ap", 0, 0), ("ap", 0, 1), ("ap", 0, 2), ("ap", 0, 3), ("rstd", 1), ("stS", 1), ("ap", 1, 0), ("ap", 1, 1), ("ap", 1, 2), ("rstd", 2), ("ap", 1, 3), ("ap", 2, 0), ("ap", 2, 1), ("ap", 2, 2), ("rstd", 3), ("ap", 2, 3), ("ap", 3, 0), ("ap", 3, 1)],
-    "dve": [("eps",), ("rgV", 0), ("q", 0), ("qw", 0, 2), ("rgV", 1), ("q", 1), ("st", 0, 0), ("rgV", 2), ("rgV", 3), ("q", 2), ("q", 3), ("cast",), ("st", 0, 1), ("st", 0, 2), ("st", 0, 3), ("ag", 0), ("qw", 2, 4), ("st", 1, 0), ("st", 1, 1), ("st", 1, 2), ("st", 1, 3), ("ag", 1), ("st", 2, 0), ("st", 2, 1), ("st", 2, 2), ("st", 2, 3), ("ag", 2), ("st", 3, 0), ("stV", 2), ("st", 3, 1), ("st", 3, 2), ("st", 3, 3), ("ag", 3), ("stV", 3), ("apV", 3, 2), ("rlV", 3, 2), ("apV", 3, 3), ("rlV", 3, 3)],
+    "act": [("warm",), ("evacS", 0), ("rgS", 0), ("evacS", 1), ("ldgb",), ("rgS", 1), ("rgS", 2), ("rgS", 3), ("evacS", 2), ("evacS", 3), ("rstd", 0), ("stS", 0), ("ap", 0, 0), ("ap", 0, 1), ("ap", 0, 2), ("ap", 0, 3), ("rstd", 1), ("stS", 1), ("ap", 1, 0), ("ap", 1, 1), ("ap", 1, 2), ("rstd", 2), ("ap", 1, 3), ("ap", 2, 0), ("ap", 2, 1), ("ap", 2, 2), ("rstd", 3), ("ap", 2, 3), ("ap", 3, 0), ("ap", 3, 1), ("ap", 3, 2)],
+    "dve": [("eps",), ("rgV", 0), ("q", 0), ("qw", 0, 2), ("rgV", 1), ("q", 1), ("st", 0, 0), ("rgV", 2), ("rgV", 3), ("q", 2), ("q", 3), ("cast",), ("st", 0, 1), ("st", 0, 2), ("st", 0, 3), ("ag", 0), ("qw", 2, 4), ("st", 1, 0), ("st", 1, 1), ("st", 1, 2), ("st", 1, 3), ("ag", 1), ("st", 2, 0), ("st", 2, 1), ("st", 2, 2), ("st", 2, 3), ("ag", 2), ("st", 3, 0), ("stV", 2), ("st", 3, 1), ("st", 3, 2), ("st", 3, 3), ("ag", 3), ("stV", 3), ("apV", 3, 3), ("rlV", 3, 3)],
     "pool": [("ident",)],
 }
 

@@ -15,20 +15,12 @@ ALU = mybir.AluOpType
 
 P = 128
 HEADS = 4
-BATCH = 4
+SAMPLES = 4
 D = 512
-MT = 4
+BLOCKS = 4
 EPS = 1e-5
-
-V_COLS = (352,288,224,256)
-V_APPLY = ()
-ORDER = {
-    "sync": [("ldw", 0), ("ldr", 0), ("ldr", 1), ("ldr", 2), ("ldr", 3), ("ldw", 1), ("so", 0, 0), ("so", 0, 1), ("so", 0, 2), ("so", 0, 3), ("so", 1, 0), ("so", 1, 1), ("so", 1, 2), ("so", 1, 3), ("so", 2, 0), ("so", 2, 1), ("so", 2, 2), ("so", 2, 3), ("so", 3, 0), ("so", 3, 1), ("so", 3, 3), ("so", 3, 2)],
-    "pe": [("tr", 0), ("tr", 1), ("mm", 0, 0), ("mm", 1, 0), ("mm", 0, 1), ("mm", 1, 1), ("tr", 2), ("tr", 3), ("mm", 0, 2), ("mm", 0, 3), ("mm", 1, 2), ("mm", 1, 3), ("mm", 2, 0), ("mm", 2, 1), ("mm", 2, 2), ("mm", 2, 3), ("mm", 3, 0), ("mm", 3, 1), ("mm", 3, 2), ("mm", 3, 3)],
-    "act": [("warm",), ("evacS", 0), ("rgS", 0), ("evacS", 1), ("ldgb",), ("rgS", 1), ("rgS", 2), ("rgS", 3), ("evacS", 2), ("evacS", 3), ("rstd", 0), ("stS", 0), ("ap", 0, 0), ("ap", 0, 1), ("ap", 0, 2), ("ap", 0, 3), ("rstd", 1), ("stS", 1), ("ap", 1, 0), ("ap", 1, 1), ("ap", 1, 2), ("rstd", 2), ("ap", 1, 3), ("ap", 2, 0), ("ap", 2, 1), ("ap", 2, 2), ("rstd", 3), ("ap", 2, 3), ("ap", 3, 0), ("ap", 3, 1), ("ap", 3, 2)],
-    "dve": [("eps",), ("rgV", 0), ("q", 0), ("qw", 0, 2), ("rgV", 1), ("q", 1), ("st", 0, 0), ("rgV", 2), ("rgV", 3), ("q", 2), ("q", 3), ("cast",), ("st", 0, 1), ("st", 0, 2), ("st", 0, 3), ("ag", 0), ("qw", 2, 4), ("st", 1, 0), ("st", 1, 1), ("st", 1, 2), ("st", 1, 3), ("ag", 1), ("st", 2, 0), ("st", 2, 1), ("st", 2, 2), ("st", 2, 3), ("ag", 2), ("st", 3, 0), ("stV", 2), ("st", 3, 1), ("st", 3, 2), ("st", 3, 3), ("ag", 3), ("stV", 3), ("apV", 3, 3), ("rlV", 3, 3)],
-    "pool": [("ident",)],
-}
+BN_STATS_DIM = 6
+V_COLS = (352, 288, 224, 256)
 
 
 def tile_block_height_reducing_filtering_pb_kernel(tc, head_res, W_merge, g_m, b_m, out):
@@ -38,225 +30,205 @@ def tile_block_height_reducing_filtering_pb_kernel(tc, head_res, W_merge, g_m, b
         psum = ctx.enter_context(tc.psum_pool(name="psum", bufs=1))
         ctx.enter_context(tc.manual_schedule())
 
-        w_sb = keep.tile([P, MT, HEADS * P], BF16, name="w_sb")
-        raw = [keep.tile([P, HEADS, D], BF16, name="raw%d" % b) for b in range(BATCH)]
-        grouped = [keep.tile([P, D, HEADS], BF16, name="grouped%d" % b, align_bytes=64) for b in range(BATCH)]
-        g16 = keep.tile([P, MT], BF16, name="g16")
-        b16 = keep.tile([P, MT], BF16, name="b16")
-        g32 = keep.tile([P, MT], F32, name="g32")
-        b32 = keep.tile([P, MT], F32, name="b32")
+        w_sb = keep.tile([P, BLOCKS, HEADS * P], BF16, name="w_sb")
+        raw = [keep.tile([P, HEADS, D], BF16, name="raw%d" % b) for b in range(SAMPLES)]
+        grouped = [keep.tile([P, D, HEADS], BF16, name="grouped%d" % b, align_bytes=64) for b in range(SAMPLES)]
+        w_grouped = keep.tile([P, BLOCKS, P, HEADS], BF16, name="w_grouped", align_bytes=64)
+        w_codes = keep.tile([P, BLOCKS, P], U32, name="w_codes", align_bytes=64)
+        w_scales = keep.tile([P, BLOCKS, P], U8, name="w_scales", align_bytes=64)
+        c_codes = keep.tile([P, SAMPLES, D], U32, name="c_codes", align_bytes=64)
+        c_scales = keep.tile([P, SAMPLES, D], U8, name="c_scales", align_bytes=64)
+        gain = keep.tile([P, BLOCKS], BF16, name="gain")
+        bias = keep.tile([P, BLOCKS], BF16, name="bias")
         ident = keep.tile([P, P], BF16, name="ident")
         eps = keep.tile([P, 1], F32, name="eps")
         warm = keep.tile([P, 1], F32, name="warm")
-        gw = keep.tile([P, MT, P, HEADS], BF16, name="gw", align_bytes=64)
-        w_codes = keep.tile([P, MT, P], U32, name="w_codes", align_bytes=64)
-        w_scl = keep.tile([P, MT, P], U8, name="w_scl", align_bytes=64)
-        c_codes = keep.tile([P, BATCH, D], U32, name="c_codes", align_bytes=64)
-        c_scl = keep.tile([P, BATCH, D], U8, name="c_scl", align_bytes=64)
-        stats = [keep.tile([P, BATCH, 6], F32, name="stats%d" % m) for m in range(MT)]
-        mv = [keep.tile([P, 2], F32, name="mv%d" % m) for m in range(MT)]
-        gm = [keep.tile([P, 1], F32, name="gm%d" % m) for m in range(MT)]
-        rstd = [keep.tile([P, 1], F32, name="rstd%d" % m) for m in range(MT)]
-        s_col = [keep.tile([P, 1], F32, name="s_col%d" % m) for m in range(MT)]
-        t_col = [keep.tile([P, 1], F32, name="t_col%d" % m) for m in range(MT)]
-        o_sb = [keep.tile([P, BATCH, D], F32, name="o_sb%d" % m) for m in range(MT)]
-        wt = {}
+        stats = [keep.tile([P, SAMPLES, BN_STATS_DIM], F32, name="stats%d" % j) for j in range(BLOCKS)]
+        mean_var = [keep.tile([P, 2], F32, name="mean_var%d" % j) for j in range(BLOCKS)]
+        neg_gain_mean = [keep.tile([P, 1], F32, name="neg_gain_mean%d" % j) for j in range(BLOCKS)]
+        inv_std = [keep.tile([P, 1], F32, name="inv_std%d" % j) for j in range(BLOCKS)]
+        scale = [keep.tile([P, 1], F32, name="scale%d" % j) for j in range(BLOCKS)]
+        shift = [keep.tile([P, 1], F32, name="shift%d" % j) for j in range(BLOCKS)]
+        result = [keep.tile([P, SAMPLES, D], F32, name="result%d" % j) for j in range(BLOCKS)]
+        w_t = {}
         acc = {}
-        w_view = W_merge.rearrange("(p m) k -> p m k", m=MT)
-        out_v = out.rearrange("b (p m) d -> m p b d", m=MT)
+        w_view = W_merge.rearrange("(p j) k -> p j k", j=BLOCKS)
+        out_view = out.rearrange("b (p j) d -> j p b d", j=BLOCKS)
 
-        def regroup(copy, b, c0, c1):
-            copy(
-                out=grouped[b][:, c0:c1, :].rearrange("p (c i) t -> p c t i", i=4),
-                in_=raw[b][:, :, c0:c1].rearrange("p t (c i) -> p c t i", i=4),
+        def load_w(j0, j1):
+            nc.sync.dma_start(out=w_sb[:, j0:j1, :], in_=w_view[:, j0:j1, :])
+
+        def load_sample(b):
+            nc.sync.dma_start(out=raw[b][:], in_=head_res[:, b].rearrange("n c d -> c n d"))
+
+        def transpose_w(j):
+            w_t[j] = psum.tile([P, HEADS, P], BF16, name="w_t%d" % j, tag="bank%d" % (SAMPLES + j))
+            for t in range(HEADS):
+                nc.tensor.transpose(w_t[j][:, t, :], w_sb[:, j, t * P:(t + 1) * P], ident[:])
+
+        def copy_out_w(j):
+            nc.scalar.copy(out=w_grouped[:, j, :, :], in_=w_t[j][:].rearrange("p t o -> p o t"))
+
+        def quantise_w(j0, j1):
+            nc.vector.quantize_mx(
+                out=w_codes[:, j0:j1, :].rearrange("p j o -> p (j o)").bitcast(FP8X4),
+                scales=w_scales[:, j0:j1, :].rearrange("p j o -> p (j o)"),
+                in_=w_grouped[:, j0:j1, :, :].rearrange("p j o t -> p (j o t)"),
             )
 
-        def run(op):
-            kind = op[0]
-            if kind == "ldw":
-                h = op[1]
-                nc.sync.dma_start(out=w_sb[:, 2 * h:2 * h + 2, :], in_=w_view[:, 2 * h:2 * h + 2, :])
-            elif kind == "ldr":
-                b = op[1]
-                nc.sync.dma_start(out=raw[b][:], in_=head_res[:, b].rearrange("n c d -> c n d"))
-            elif kind == "ldgb":
-                nc.scalar.dma_start(out=g16[:], in_=g_m.rearrange("(p m) -> p m", m=MT))
-                nc.scalar.dma_start(out=b16[:], in_=b_m.rearrange("(p m) -> p m", m=MT))
-            elif kind == "ident":
-                make_identity(nc, ident[:])
-            elif kind == "eps":
-                nc.vector.memset(eps[:], EPS)
-            elif kind == "warm":
-                nc.scalar.activation(out=warm[:], in_=eps[:], func=ACT.Abs_reciprocal_sqrt)
-            elif kind == "cast":
-                nc.vector.tensor_copy(out=g32[:], in_=g16[:])
-                nc.vector.tensor_copy(out=b32[:], in_=b16[:])
-            elif kind == "tr":
-                m = op[1]
-                wt[m] = psum.tile([P, HEADS, P], BF16, name="wt%d" % m, tag="bank%d" % (4 + m))
-                for t in range(HEADS):
-                    nc.tensor.transpose(wt[m][:, t, :], w_sb[:, m, t * P:(t + 1) * P], ident[:])
-            elif kind == "evacS" or kind == "evacV":
-                m = op[1]
-                copy = nc.scalar.copy if kind == "evacS" else nc.vector.tensor_copy
-                copy(out=gw[:, m, :, :], in_=wt[m][:].rearrange("p t o -> p o t"))
-            elif kind == "qw":
-                m0, m1 = op[1], op[2]
-                nc.vector.quantize_mx(
-                    out=w_codes[:, m0:m1, :].rearrange("p m o -> p (m o)").bitcast(FP8X4),
-                    scales=w_scl[:, m0:m1, :].rearrange("p m o -> p (m o)"),
-                    in_=gw[:, m0:m1, :, :].rearrange("p m o t -> p (m o t)"),
-                )
-            elif kind == "rgV":
-                regroup(nc.vector.tensor_copy, op[1], 0, V_COLS[op[1]])
-            elif kind == "rgS":
-                regroup(nc.scalar.copy, op[1], V_COLS[op[1]], D)
-            elif kind == "q":
-                b = op[1]
-                nc.vector.quantize_mx(
-                    out=c_codes[:, b, :].bitcast(FP8X4),
-                    scales=c_scl[:, b, :],
-                    in_=grouped[b][:].rearrange("p w j -> p (w j)"),
-                )
-            elif kind == "mm":
-                m, b = op[1], op[2]
-                acc[(m, b)] = psum.tile([P, D], F32, name="acc%d_%d" % (m, b), tag="bank%d" % (4 * (m % 2) + b))
-                nc.tensor.matmul_mx(
-                    out=acc[(m, b)][:],
-                    lhsT=w_codes[:, m, :].bitcast(FP8X4),
-                    lhsT_scale=w_scl[:, m, :],
-                    rhs=c_codes[:, b, :].bitcast(FP8X4),
-                    rhs_scale=c_scl[:, b, :],
-                    start=True,
-                    stop=True,
-                )
-            elif kind == "st":
-                m, b = op[1], op[2]
-                nc.vector.bn_stats(out=stats[m][:, b, :], in_=acc[(m, b)][:])
-            elif kind == "ag":
-                m = op[1]
-                nc.vector.bn_aggr(out=mv[m][:], in_=stats[m][:].rearrange("p b s -> p (b s)"))
-                nc.vector.scalar_tensor_tensor(
-                    out=gm[m][:], in0=mv[m][:, 0:1], scalar=-1.0, in1=g32[:, m:m + 1], op0=ALU.mult, op1=ALU.mult
-                )
-            elif kind == "rstd":
-                m = op[1]
-                nc.scalar.activation(
-                    out=rstd[m][:], in_=mv[m][:, 1:2], func=ACT.Abs_reciprocal_sqrt, bias=eps[:, 0:1]
-                )
-            elif kind == "stS":
-                m = op[1]
-                nc.scalar.activation(out=s_col[m][:], in_=g32[:, m:m + 1], func=ACT.Copy, scale=rstd[m][:, 0:1])
-                nc.scalar.activation(
-                    out=t_col[m][:], in_=gm[m][:], func=ACT.Identity, scale=rstd[m][:, 0:1], bias=b32[:, m:m + 1]
-                )
-            elif kind == "stV":
-                m = op[1]
-                nc.vector.tensor_mul(out=s_col[m][:], in0=g32[:, m:m + 1], in1=rstd[m][:])
-                nc.vector.scalar_tensor_tensor(
-                    out=t_col[m][:], in0=gm[m][:], scalar=rstd[m][:, 0:1], in1=b32[:, m:m + 1],
-                    op0=ALU.mult, op1=ALU.add,
-                )
-            elif kind == "ap":
-                m, b = op[1], op[2]
-                nc.scalar.activation(
-                    out=o_sb[m][:, b, :], in_=acc[(m, b)][:], func=ACT.Relu,
-                    scale=s_col[m][:, 0:1], bias=t_col[m][:, 0:1],
-                )
-            elif kind == "apV":
-                m, b = op[1], op[2]
-                nc.vector.tensor_scalar(
-                    out=o_sb[m][:, b, :], in0=acc[(m, b)][:], scalar1=s_col[m][:, 0:1], scalar2=t_col[m][:, 0:1],
-                    op0=ALU.mult, op1=ALU.add,
-                )
-            elif kind == "rlV":
-                m, b = op[1], op[2]
-                nc.vector.tensor_scalar_max(out=o_sb[m][:, b, :], in0=o_sb[m][:, b, :], scalar1=0.0)
-            elif kind == "rlG":
-                m, b = op[1], op[2]
-                nc.gpsimd.tensor_scalar(
-                    out=o_sb[m][:, b, :], in0=o_sb[m][:, b, :], scalar1=0.0, scalar2=0.0, op0=ALU.max, op1=ALU.add
-                )
-            elif kind == "so":
-                m, b = op[1], op[2]
-                nc.sync.dma_start(out=out_v[m][:, b, :], in_=o_sb[m][:, b, :])
-            else:
-                raise ValueError(kind)
+        def regroup(copy, b, d0, d1):
+            copy(
+                out=grouped[b][:, d0:d1, :].rearrange("p (c i) t -> p c t i", i=4),
+                in_=raw[b][:, :, d0:d1].rearrange("p t (c i) -> p c t i", i=4),
+            )
 
-        def needs(op):
-            kind = op[0]
-            if kind == "warm":
-                return [("eps",)]
-            if kind == "cast":
-                return [("ldgb",)]
-            if kind == "tr":
-                return [("ldw", op[1] // 2), ("ident",)]
-            if kind == "evacS" or kind == "evacV":
-                return [("tr", op[1])]
-            if kind == "qw":
-                return [("evac", m) for m in range(op[1], op[2])]
-            if kind == "rgV" or kind == "rgS":
-                return [("ldr", op[1])]
-            if kind == "q":
-                return [("rgV", op[1]), ("rgS", op[1])]
-            if kind == "mm":
-                m, b = op[1], op[2]
-                first = [("qwm", m), ("q", b)]
-                if m == 1:
-                    first.append(("evac", b))
-                if m >= 2:
-                    first.append(("applied", m - 2, b))
-                return first
-            if kind == "st":
-                return [("mm", op[1], op[2])]
-            if kind == "ag":
-                return [("st", op[1], b) for b in range(BATCH)] + [("cast",)]
-            if kind == "rstd":
-                return [("ag", op[1]), ("eps",)]
-            if kind == "stS" or kind == "stV":
-                return [("rstd", op[1])]
-            if kind == "ap" or kind == "apV":
-                return [("scale", op[1]), ("st", op[1], op[2])]
-            if kind == "rlV" or kind == "rlG":
-                return [("apV", op[1], op[2])]
-            if kind == "so":
-                return [("ready", op[1], op[2])]
-            return []
+        def quantise(b):
+            nc.vector.quantize_mx(
+                out=c_codes[:, b, :].bitcast(FP8X4),
+                scales=c_scales[:, b, :],
+                in_=grouped[b][:].rearrange("p d t -> p (d t)"),
+            )
 
-        def gives(op):
-            kind = op[0]
-            made = [op]
-            if kind == "evacS" or kind == "evacV":
-                made.append(("evac", op[1]))
-            if kind == "qw":
-                made.extend([("qwm", m) for m in range(op[1], op[2])])
-            if kind == "stS" or kind == "stV":
-                made.append(("scale", op[1]))
-            if kind == "ap":
-                made.extend([("applied", op[1], op[2]), ("ready", op[1], op[2])])
-            if kind == "apV":
-                made.append(("applied", op[1], op[2]))
-            if kind == "rlV" or kind == "rlG":
-                made.append(("ready", op[1], op[2]))
-            return made
+        def mx_pass(j, b):
+            acc[(j, b)] = psum.tile([P, D], F32, name="acc%d_%d" % (j, b), tag="bank%d" % (SAMPLES * (j % 2) + b))
+            nc.tensor.matmul_mx(
+                out=acc[(j, b)][:],
+                lhsT=w_codes[:, j, :].bitcast(FP8X4),
+                lhsT_scale=w_scales[:, j, :],
+                rhs=c_codes[:, b, :].bitcast(FP8X4),
+                rhs_scale=c_scales[:, b, :],
+                start=True,
+                stop=True,
+            )
 
-        done = set()
-        for b in range(BATCH):
-            if V_COLS[b] == 0:
-                done.add(("rgV", b))
-            if V_COLS[b] == D:
-                done.add(("rgS", b))
-        pos = dict((e, 0) for e in ORDER)
-        left = sum(len(ORDER[e]) for e in ORDER)
-        while left > 0:
-            moved = False
-            for e in ("sync", "pool", "pe", "dve", "act"):
-                while pos[e] < len(ORDER[e]) and all(n in done for n in needs(ORDER[e][pos[e]])):
-                    op = ORDER[e][pos[e]]
-                    run(op)
-                    for k in gives(op):
-                        done.add(k)
-                    pos[e] += 1
-                    left -= 1
-                    moved = True
-            assert moved, "the engines' orders wait for each other"
+        def statistics(j, b):
+            nc.vector.bn_stats(out=stats[j][:, b, :], in_=acc[(j, b)][:])
+
+        def aggregate(j):
+            nc.vector.bn_aggr(out=mean_var[j][:], in_=stats[j][:].rearrange("p b s -> p (b s)"))
+            nc.vector.scalar_tensor_tensor(
+                out=neg_gain_mean[j][:], in0=mean_var[j][:, 0:1], scalar=-1.0, in1=gain[:, j:j + 1],
+                op0=ALU.mult, op1=ALU.mult,
+            )
+
+        def inverse_std(j):
+            nc.scalar.activation(
+                out=inv_std[j][:], in_=mean_var[j][:, 1:2], func=ACT.Abs_reciprocal_sqrt, bias=eps[:, 0:1]
+            )
+
+        def scale_shift_on_scalar(j):
+            nc.scalar.activation(out=scale[j][:], in_=gain[:, j:j + 1], func=ACT.Copy, scale=inv_std[j][:, 0:1])
+            nc.scalar.activation(
+                out=shift[j][:], in_=neg_gain_mean[j][:], func=ACT.Identity,
+                scale=inv_std[j][:, 0:1], bias=bias[:, j:j + 1],
+            )
+
+        def scale_shift_on_vector(j):
+            nc.vector.tensor_mul(out=scale[j][:], in0=gain[:, j:j + 1], in1=inv_std[j][:])
+            nc.vector.scalar_tensor_tensor(
+                out=shift[j][:], in0=neg_gain_mean[j][:], scalar=inv_std[j][:, 0:1], in1=bias[:, j:j + 1],
+                op0=ALU.mult, op1=ALU.add,
+            )
+
+        def apply_on_scalar(j, b):
+            nc.scalar.activation(
+                out=result[j][:, b, :], in_=acc[(j, b)][:], func=ACT.Relu,
+                scale=scale[j][:, 0:1], bias=shift[j][:, 0:1],
+            )
+
+        def apply_on_vector(j, b):
+            nc.vector.tensor_scalar(
+                out=result[j][:, b, :], in0=acc[(j, b)][:], scalar1=scale[j][:, 0:1], scalar2=shift[j][:, 0:1],
+                op0=ALU.mult, op1=ALU.add,
+            )
+            nc.vector.tensor_scalar_max(out=result[j][:, b, :], in0=result[j][:, b, :], scalar1=0.0)
+
+        def store(j, b):
+            nc.sync.dma_start(out=out_view[j][:, b, :], in_=result[j][:, b, :])
+
+        load_w(0, 2)
+        for b in range(SAMPLES):
+            load_sample(b)
+        load_w(2, 4)
+        make_identity(nc, ident[:])
+        nc.vector.memset(eps[:], EPS)
+        nc.scalar.activation(out=warm[:], in_=eps[:], func=ACT.Abs_reciprocal_sqrt)
+
+        transpose_w(0)
+        transpose_w(1)
+        copy_out_w(0)
+        regroup(nc.scalar.copy, 0, V_COLS[0], D)
+        copy_out_w(1)
+        nc.scalar.dma_start(out=gain[:], in_=g_m.rearrange("(p j) -> p j", j=BLOCKS))
+        nc.scalar.dma_start(out=bias[:], in_=b_m.rearrange("(p j) -> p j", j=BLOCKS))
+        regroup(nc.vector.tensor_copy, 0, 0, V_COLS[0])
+        quantise(0)
+        quantise_w(0, 2)
+        mx_pass(0, 0)
+        mx_pass(1, 0)
+        regroup(nc.scalar.copy, 1, V_COLS[1], D)
+        regroup(nc.vector.tensor_copy, 1, 0, V_COLS[1])
+        quantise(1)
+        statistics(0, 0)
+        mx_pass(0, 1)
+        mx_pass(1, 1)
+        transpose_w(2)
+        transpose_w(3)
+        for b in (2, 3):
+            regroup(nc.scalar.copy, b, V_COLS[b], D)
+        for b in (2, 3):
+            regroup(nc.vector.tensor_copy, b, 0, V_COLS[b])
+        quantise(2)
+        quantise(3)
+        mx_pass(0, 2)
+        mx_pass(0, 3)
+        for b in (1, 2, 3):
+            statistics(0, b)
+        aggregate(0)
+        copy_out_w(2)
+        copy_out_w(3)
+        quantise_w(2, 4)
+        mx_pass(1, 2)
+        mx_pass(1, 3)
+
+        inverse_std(0)
+        scale_shift_on_scalar(0)
+        for b in range(SAMPLES):
+            apply_on_scalar(0, b)
+            store(0, b)
+            mx_pass(2, b)
+        for b in range(SAMPLES):
+            statistics(1, b)
+        aggregate(1)
+        inverse_std(1)
+        scale_shift_on_scalar(1)
+        for b in range(SAMPLES - 1):
+            apply_on_scalar(1, b)
+            store(1, b)
+            mx_pass(3, b)
+        for b in range(SAMPLES):
+            statistics(2, b)
+        aggregate(2)
+        inverse_std(2)
+        apply_on_scalar(1, 3)
+        store(1, 3)
+        mx_pass(3, 3)
+        statistics(3, 0)
+        scale_shift_on_vector(2)
+        for b in range(SAMPLES - 1):
+            apply_on_scalar(2, b)
+            store(2, b)
+        for b in (1, 2, 3):
+            statistics(3, b)
+        aggregate(3)
+        inverse_std(3)
+        apply_on_scalar(2, 3)
+        store(2, 3)
+        scale_shift_on_vector(3)
+        apply_on_vector(3, 3)
+        for b in (0, 1):
+            apply_on_scalar(3, b)
+            store(3, b)
+        store(3, 3)
+        apply_on_scalar(3, 2)
+        store(3, 2)

@@ -58,8 +58,8 @@ def tile_block_height_reducing_filtering_pb_kernel(tc, head_res, W_merge, g_m, b
         def load_w(j0, j1):
             nc.sync.dma_start(out=w_sb[:, j0:j1, :], in_=w_view[:, j0:j1, :])
 
-        def load_sample(b):
-            nc.sync.dma_start(out=raw[b][:], in_=head_res[:, b].rearrange("n c d -> c n d"))
+        def load_sample(b, d0=0, d1=D):
+            nc.sync.dma_start(out=raw[b][:, :, d0:d1], in_=head_res[:, b, :, d0:d1].rearrange("n c d -> c n d"))
 
         def transpose_w(j):
             w_t[j] = psum.tile([P, HEADS, P], BF16, name="w_t%d" % j, tag="bank%d" % (SAMPLES + j))
@@ -82,11 +82,11 @@ def tile_block_height_reducing_filtering_pb_kernel(tc, head_res, W_merge, g_m, b
                 in_=raw[b][:, :, d0:d1].rearrange("p t (c i) -> p c t i", i=4),
             )
 
-        def quantise(b):
+        def quantise(b, d0=0, d1=D):
             nc.vector.quantize_mx(
-                out=c_codes[:, b, :].bitcast(FP8X4),
-                scales=c_scales[:, b, :],
-                in_=grouped[b][:].rearrange("p d t -> p (d t)"),
+                out=c_codes[:, b, d0:d1].bitcast(FP8X4),
+                scales=c_scales[:, b, d0:d1],
+                in_=grouped[b][:, d0:d1, :].rearrange("p d t -> p (d t)"),
             )
 
         def mx_pass(j, b):
@@ -147,8 +147,10 @@ def tile_block_height_reducing_filtering_pb_kernel(tc, head_res, W_merge, g_m, b
             nc.sync.dma_start(out=out_view[j][:, b, :], in_=result[j][:, b, :])
 
         load_w(0, 2)
-        for b in range(SAMPLES):
+        for b in range(SAMPLES - 1):
             load_sample(b)
+        load_sample(3, 0, 256)
+        load_sample(3, 256, D)
         load_w(2, 4)
         make_identity(nc, ident[:])
         nc.vector.memset(eps[:], EPS)
@@ -174,12 +176,15 @@ def tile_block_height_reducing_filtering_pb_kernel(tc, head_res, W_merge, g_m, b
         mx_pass(1, 1)
         transpose_w(2)
         transpose_w(3)
-        for b in (2, 3):
-            regroup(nc.scalar.copy, b, V_COLS[b], D)
-        for b in (2, 3):
-            regroup(nc.vector.tensor_copy, b, 0, V_COLS[b])
+        regroup(nc.scalar.copy, 2, V_COLS[2], D)
+        regroup(nc.scalar.copy, 3, 128, 256)
+        regroup(nc.scalar.copy, 3, 256 + 168, D)
+        regroup(nc.vector.tensor_copy, 2, 0, V_COLS[2])
+        regroup(nc.vector.tensor_copy, 3, 0, 128)
         quantise(2)
-        quantise(3)
+        quantise(3, 0, 256)
+        regroup(nc.vector.tensor_copy, 3, 256, 256 + 168)
+        quantise(3, 256, D)
         mx_pass(0, 2)
         mx_pass(0, 3)
         for b in (1, 2, 3):

@@ -39,7 +39,7 @@ def tile_block_height_reducing_filtering_pb_kernel(tc, head_res, W_merge, g_m, b
         c_codes = keep.tile([P, SAMPLES, D], U32, name="c_codes", align_bytes=64)
         c_scales = keep.tile([P, SAMPLES, D], U8, name="c_scales", align_bytes=64)
         gain = keep.tile([P, BLOCKS], BF16, name="gain")
-        bias = keep.tile([P, BLOCKS], BF16, name="bias")
+        offset = keep.tile([P, BLOCKS], BF16, name="offset")
         ident = keep.tile([P, P], BF16, name="ident")
         eps = keep.tile([P, 1], F32, name="eps")
         warm = keep.tile([P, 1], F32, name="warm")
@@ -47,8 +47,8 @@ def tile_block_height_reducing_filtering_pb_kernel(tc, head_res, W_merge, g_m, b
         mean_var = [keep.tile([P, 2], F32, name="mean_var%d" % j) for j in range(BLOCKS)]
         neg_gain_mean = [keep.tile([P, 1], F32, name="neg_gain_mean%d" % j) for j in range(BLOCKS)]
         inv_std = [keep.tile([P, 1], F32, name="inv_std%d" % j) for j in range(BLOCKS)]
-        scale = [keep.tile([P, 1], F32, name="scale%d" % j) for j in range(BLOCKS)]
-        shift = [keep.tile([P, 1], F32, name="shift%d" % j) for j in range(BLOCKS)]
+        bn_scale = [keep.tile([P, 1], F32, name="bn_scale%d" % j) for j in range(BLOCKS)]
+        bn_shift = [keep.tile([P, 1], F32, name="bn_shift%d" % j) for j in range(BLOCKS)]
         result = [keep.tile([P, SAMPLES, D], F32, name="result%d" % j) for j in range(BLOCKS)]
         w_t = {}
         acc = {}
@@ -58,8 +58,8 @@ def tile_block_height_reducing_filtering_pb_kernel(tc, head_res, W_merge, g_m, b
         def load_w(j0, j1):
             nc.sync.dma_start(out=w_sb[:, j0:j1, :], in_=w_view[:, j0:j1, :])
 
-        def load_sample(b, d0=0, d1=D):
-            nc.sync.dma_start(out=raw[b][:, :, d0:d1], in_=head_res[:, b, :, d0:d1].rearrange("n c d -> c n d"))
+        def load_sample(b):
+            nc.sync.dma_start(out=raw[b][:], in_=head_res[:, b].rearrange("n c d -> c n d"))
 
         def transpose_w(j):
             w_t[j] = psum.tile([P, HEADS, P], BF16, name="w_t%d" % j, tag="bank%d" % (SAMPLES + j))
@@ -67,26 +67,26 @@ def tile_block_height_reducing_filtering_pb_kernel(tc, head_res, W_merge, g_m, b
                 nc.tensor.transpose(w_t[j][:, t, :], w_sb[:, j, t * P:(t + 1) * P], ident[:])
 
         def copy_out_w(j):
-            nc.scalar.copy(out=w_grouped[:, j, :, :], in_=w_t[j][:].rearrange("p t o -> p o t"))
+            nc.scalar.copy(out=w_grouped[:, j, :, :], in_=w_t[j][:].rearrange("p t i -> p i t"))
 
         def quantise_w(j0, j1):
             nc.vector.quantize_mx(
-                out=w_codes[:, j0:j1, :].rearrange("p j o -> p (j o)").bitcast(FP8X4),
-                scales=w_scales[:, j0:j1, :].rearrange("p j o -> p (j o)"),
-                in_=w_grouped[:, j0:j1, :, :].rearrange("p j o t -> p (j o t)"),
+                out=w_codes[:, j0:j1, :].rearrange("p j i -> p (j i)").bitcast(FP8X4),
+                scales=w_scales[:, j0:j1, :].rearrange("p j i -> p (j i)"),
+                in_=w_grouped[:, j0:j1, :, :].rearrange("p j i t -> p (j i t)"),
             )
 
         def regroup(copy, b, d0, d1):
             copy(
-                out=grouped[b][:, d0:d1, :].rearrange("p (c i) t -> p c t i", i=4),
-                in_=raw[b][:, :, d0:d1].rearrange("p t (c i) -> p c t i", i=4),
+                out=grouped[b][:, d0:d1, :].rearrange("p (g r) t -> p g t r", r=4),
+                in_=raw[b][:, :, d0:d1].rearrange("p t (g r) -> p g t r", r=4),
             )
 
-        def quantise(b, d0=0, d1=D):
+        def quantise(b):
             nc.vector.quantize_mx(
-                out=c_codes[:, b, d0:d1].bitcast(FP8X4),
-                scales=c_scales[:, b, d0:d1],
-                in_=grouped[b][:, d0:d1, :].rearrange("p d t -> p (d t)"),
+                out=c_codes[:, b, :].bitcast(FP8X4),
+                scales=c_scales[:, b, :],
+                in_=grouped[b][:].rearrange("p d t -> p (d t)"),
             )
 
         def mx_pass(j, b):
@@ -117,28 +117,28 @@ def tile_block_height_reducing_filtering_pb_kernel(tc, head_res, W_merge, g_m, b
             )
 
         def scale_shift_on_scalar(j):
-            nc.scalar.activation(out=scale[j][:], in_=gain[:, j:j + 1], func=ACT.Copy, scale=inv_std[j][:, 0:1])
+            nc.scalar.activation(out=bn_scale[j][:], in_=gain[:, j:j + 1], func=ACT.Copy, scale=inv_std[j][:, 0:1])
             nc.scalar.activation(
-                out=shift[j][:], in_=neg_gain_mean[j][:], func=ACT.Identity,
-                scale=inv_std[j][:, 0:1], bias=bias[:, j:j + 1],
+                out=bn_shift[j][:], in_=neg_gain_mean[j][:], func=ACT.Identity,
+                scale=inv_std[j][:, 0:1], bias=offset[:, j:j + 1],
             )
 
         def scale_shift_on_vector(j):
-            nc.vector.tensor_mul(out=scale[j][:], in0=gain[:, j:j + 1], in1=inv_std[j][:])
+            nc.vector.tensor_mul(out=bn_scale[j][:], in0=gain[:, j:j + 1], in1=inv_std[j][:])
             nc.vector.scalar_tensor_tensor(
-                out=shift[j][:], in0=neg_gain_mean[j][:], scalar=inv_std[j][:, 0:1], in1=bias[:, j:j + 1],
+                out=bn_shift[j][:], in0=neg_gain_mean[j][:], scalar=inv_std[j][:, 0:1], in1=offset[:, j:j + 1],
                 op0=ALU.mult, op1=ALU.add,
             )
 
         def apply_on_scalar(j, b):
             nc.scalar.activation(
                 out=result[j][:, b, :], in_=acc[(j, b)][:], func=ACT.Relu,
-                scale=scale[j][:, 0:1], bias=shift[j][:, 0:1],
+                scale=bn_scale[j][:, 0:1], bias=bn_shift[j][:, 0:1],
             )
 
         def apply_on_vector(j, b):
             nc.vector.tensor_scalar(
-                out=result[j][:, b, :], in0=acc[(j, b)][:], scalar1=scale[j][:, 0:1], scalar2=shift[j][:, 0:1],
+                out=result[j][:, b, :], in0=acc[(j, b)][:], scalar1=bn_scale[j][:, 0:1], scalar2=bn_shift[j][:, 0:1],
                 op0=ALU.mult, op1=ALU.add,
             )
             nc.vector.tensor_scalar_max(out=result[j][:, b, :], in0=result[j][:, b, :], scalar1=0.0)
@@ -147,10 +147,8 @@ def tile_block_height_reducing_filtering_pb_kernel(tc, head_res, W_merge, g_m, b
             nc.sync.dma_start(out=out_view[j][:, b, :], in_=result[j][:, b, :])
 
         load_w(0, 2)
-        for b in range(SAMPLES - 1):
+        for b in range(SAMPLES):
             load_sample(b)
-        load_sample(3, 0, 256)
-        load_sample(3, 256, D)
         load_w(2, 4)
         make_identity(nc, ident[:])
         nc.vector.memset(eps[:], EPS)
@@ -162,7 +160,7 @@ def tile_block_height_reducing_filtering_pb_kernel(tc, head_res, W_merge, g_m, b
         regroup(nc.scalar.copy, 0, V_COLS[0], D)
         copy_out_w(1)
         nc.scalar.dma_start(out=gain[:], in_=g_m.rearrange("(p j) -> p j", j=BLOCKS))
-        nc.scalar.dma_start(out=bias[:], in_=b_m.rearrange("(p j) -> p j", j=BLOCKS))
+        nc.scalar.dma_start(out=offset[:], in_=b_m.rearrange("(p j) -> p j", j=BLOCKS))
         regroup(nc.vector.tensor_copy, 0, 0, V_COLS[0])
         quantise(0)
         quantise_w(0, 2)
@@ -176,15 +174,12 @@ def tile_block_height_reducing_filtering_pb_kernel(tc, head_res, W_merge, g_m, b
         mx_pass(1, 1)
         transpose_w(2)
         transpose_w(3)
-        regroup(nc.scalar.copy, 2, V_COLS[2], D)
-        regroup(nc.scalar.copy, 3, 128, 256)
-        regroup(nc.scalar.copy, 3, 256 + 168, D)
-        regroup(nc.vector.tensor_copy, 2, 0, V_COLS[2])
-        regroup(nc.vector.tensor_copy, 3, 0, 128)
+        for b in (2, 3):
+            regroup(nc.scalar.copy, b, V_COLS[b], D)
+        for b in (2, 3):
+            regroup(nc.vector.tensor_copy, b, 0, V_COLS[b])
         quantise(2)
-        quantise(3, 0, 256)
-        regroup(nc.vector.tensor_copy, 3, 256, 256 + 168)
-        quantise(3, 256, D)
+        quantise(3)
         mx_pass(0, 2)
         mx_pass(0, 3)
         for b in (1, 2, 3):

from contextlib import ExitStack

import concourse.mybir as mybir
from concourse.masks import make_identity

FLOPS = 2 * 512 * 512 * 2048

F32 = mybir.dt.float32
BF16 = mybir.dt.bfloat16
U32 = mybir.dt.uint32
U8 = mybir.dt.uint8
FP8X4 = mybir.dt.float8_e4m3fn_x4
ACT = mybir.ActivationFunctionType
ALU = mybir.AluOpType

P = 128
HEADS = 4
SAMPLES = 4
D = 512
BLOCKS = 4
EPS = 1e-5
BN_STATS_DIM = 6
V_COLS = (352, 288, 224, 256)


def tile_block_height_reducing_filtering_pb_kernel(tc, head_res, W_merge, g_m, b_m, out):
    nc = tc.nc
    with ExitStack() as ctx:
        keep = ctx.enter_context(tc.tile_pool(name="keep", bufs=1))
        psum = ctx.enter_context(tc.psum_pool(name="psum", bufs=1))
        ctx.enter_context(tc.manual_schedule())

        w_sb = keep.tile([P, BLOCKS, HEADS * P], BF16, name="w_sb")
        raw = [keep.tile([P, HEADS, D], BF16, name="raw%d" % b) for b in range(SAMPLES)]
        grouped = [keep.tile([P, D, HEADS], BF16, name="grouped%d" % b, align_bytes=64) for b in range(SAMPLES)]
        w_grouped = keep.tile([P, BLOCKS, P, HEADS], BF16, name="w_grouped", align_bytes=64)
        w_codes = keep.tile([P, BLOCKS, P], U32, name="w_codes", align_bytes=64)
        w_scales = keep.tile([P, BLOCKS, P], U8, name="w_scales", align_bytes=64)
        c_codes = keep.tile([P, SAMPLES, D], U32, name="c_codes", align_bytes=64)
        c_scales = keep.tile([P, SAMPLES, D], U8, name="c_scales", align_bytes=64)
        gain = keep.tile([P, BLOCKS], BF16, name="gain")
        offset = keep.tile([P, BLOCKS], BF16, name="offset")
        ident = keep.tile([P, P], BF16, name="ident")
        eps = keep.tile([P, 1], F32, name="eps")
        warm = keep.tile([P, 1], F32, name="warm")
        stats = [keep.tile([P, SAMPLES, BN_STATS_DIM], F32, name="stats%d" % j) for j in range(BLOCKS)]
        mean_var = [keep.tile([P, 2], F32, name="mean_var%d" % j) for j in range(BLOCKS)]
        neg_gain_mean = [keep.tile([P, 1], F32, name="neg_gain_mean%d" % j) for j in range(BLOCKS)]
        inv_std = [keep.tile([P, 1], F32, name="inv_std%d" % j) for j in range(BLOCKS)]
        bn_scale = [keep.tile([P, 1], F32, name="bn_scale%d" % j) for j in range(BLOCKS)]
        bn_shift = [keep.tile([P, 1], F32, name="bn_shift%d" % j) for j in range(BLOCKS)]
        result = [keep.tile([P, SAMPLES, D], F32, name="result%d" % j) for j in range(BLOCKS)]
        w_t = {}
        acc = {}
        w_view = W_merge.rearrange("(p j) k -> p j k", j=BLOCKS)
        out_view = out.rearrange("b (p j) d -> j p b d", j=BLOCKS)

        def load_w(j0, j1):
            nc.sync.dma_start(out=w_sb[:, j0:j1, :], in_=w_view[:, j0:j1, :])

        def load_sample(b):
            nc.sync.dma_start(out=raw[b][:], in_=head_res[:, b].rearrange("n c d -> c n d"))

        def transpose_w(j):
            w_t[j] = psum.tile([P, HEADS, P], BF16, name="w_t%d" % j, tag="bank%d" % (SAMPLES + j))
            for t in range(HEADS):
                nc.tensor.transpose(w_t[j][:, t, :], w_sb[:, j, t * P:(t + 1) * P], ident[:])

        def copy_out_w(j):
            nc.scalar.copy(out=w_grouped[:, j, :, :], in_=w_t[j][:].rearrange("p t i -> p i t"))

        def quantise_w(j0, j1):
            nc.vector.quantize_mx(
                out=w_codes[:, j0:j1, :].rearrange("p j i -> p (j i)").bitcast(FP8X4),
                scales=w_scales[:, j0:j1, :].rearrange("p j i -> p (j i)"),
                in_=w_grouped[:, j0:j1, :, :].rearrange("p j i t -> p (j i t)"),
            )

        def regroup(copy, b, d0, d1):
            copy(
                out=grouped[b][:, d0:d1, :].rearrange("p (g r) t -> p g t r", r=4),
                in_=raw[b][:, :, d0:d1].rearrange("p t (g r) -> p g t r", r=4),
            )

        def quantise(b):
            nc.vector.quantize_mx(
                out=c_codes[:, b, :].bitcast(FP8X4),
                scales=c_scales[:, b, :],
                in_=grouped[b][:].rearrange("p d t -> p (d t)"),
            )

        def mx_pass(j, b):
            acc[(j, b)] = psum.tile([P, D], F32, name="acc%d_%d" % (j, b), tag="bank%d" % (SAMPLES * (j % 2) + b))
            nc.tensor.matmul_mx(
                out=acc[(j, b)][:],
                lhsT=w_codes[:, j, :].bitcast(FP8X4),
                lhsT_scale=w_scales[:, j, :],
                rhs=c_codes[:, b, :].bitcast(FP8X4),
                rhs_scale=c_scales[:, b, :],
                start=True,
                stop=True,
            )

        def statistics(j, b):
            nc.vector.bn_stats(out=stats[j][:, b, :], in_=acc[(j, b)][:])

        def aggregate(j):
            nc.vector.bn_aggr(out=mean_var[j][:], in_=stats[j][:].rearrange("p b s -> p (b s)"))
            nc.vector.scalar_tensor_tensor(
                out=neg_gain_mean[j][:], in0=mean_var[j][:, 0:1], scalar=-1.0, in1=gain[:, j:j + 1],
                op0=ALU.mult, op1=ALU.mult,
            )

        def inverse_std(j):
            nc.scalar.activation(
                out=inv_std[j][:], in_=mean_var[j][:, 1:2], func=ACT.Abs_reciprocal_sqrt, bias=eps[:, 0:1]
            )

        def scale_shift_on_scalar(j):
            nc.scalar.activation(out=bn_scale[j][:], in_=gain[:, j:j + 1], func=ACT.Copy, scale=inv_std[j][:, 0:1])
            nc.scalar.activation(
                out=bn_shift[j][:], in_=neg_gain_mean[j][:], func=ACT.Identity,
                scale=inv_std[j][:, 0:1], bias=offset[:, j:j + 1],
            )

        def scale_shift_on_vector(j):
            nc.vector.tensor_mul(out=bn_scale[j][:], in0=gain[:, j:j + 1], in1=inv_std[j][:])
            nc.vector.scalar_tensor_tensor(
                out=bn_shift[j][:], in0=neg_gain_mean[j][:], scalar=inv_std[j][:, 0:1], in1=offset[:, j:j + 1],
                op0=ALU.mult, op1=ALU.add,
            )

        def apply_on_scalar(j, b):
            nc.scalar.activation(
                out=result[j][:, b, :], in_=acc[(j, b)][:], func=ACT.Relu,
                scale=bn_scale[j][:, 0:1], bias=bn_shift[j][:, 0:1],
            )

        def apply_on_vector(j, b):
            nc.vector.tensor_scalar(
                out=result[j][:, b, :], in0=acc[(j, b)][:], scalar1=bn_scale[j][:, 0:1], scalar2=bn_shift[j][:, 0:1],
                op0=ALU.mult, op1=ALU.add,
            )
            nc.vector.tensor_scalar_max(out=result[j][:, b, :], in0=result[j][:, b, :], scalar1=0.0)

        def store(j, b):
            nc.sync.dma_start(out=out_view[j][:, b, :], in_=result[j][:, b, :])

        load_w(0, 2)
        for b in range(SAMPLES):
            load_sample(b)
        load_w(2, 4)
        make_identity(nc, ident[:])
        nc.vector.memset(eps[:], EPS)
        nc.scalar.activation(out=warm[:], in_=eps[:], func=ACT.Abs_reciprocal_sqrt)

        transpose_w(0)
        transpose_w(1)
        copy_out_w(0)
        regroup(nc.scalar.copy, 0, V_COLS[0], D)
        copy_out_w(1)
        nc.scalar.dma_start(out=gain[:], in_=g_m.rearrange("(p j) -> p j", j=BLOCKS))
        nc.scalar.dma_start(out=offset[:], in_=b_m.rearrange("(p j) -> p j", j=BLOCKS))
        regroup(nc.vector.tensor_copy, 0, 0, V_COLS[0])
        quantise(0)
        quantise_w(0, 2)
        mx_pass(0, 0)
        mx_pass(1, 0)
        regroup(nc.scalar.copy, 1, V_COLS[1], D)
        regroup(nc.vector.tensor_copy, 1, 0, V_COLS[1])
        quantise(1)
        statistics(0, 0)
        mx_pass(0, 1)
        mx_pass(1, 1)
        transpose_w(2)
        transpose_w(3)
        for b in (2, 3):
            regroup(nc.scalar.copy, b, V_COLS[b], D)
        for b in (2, 3):
            regroup(nc.vector.tensor_copy, b, 0, V_COLS[b])
        quantise(2)
        quantise(3)
        mx_pass(0, 2)
        mx_pass(0, 3)
        for b in (1, 2, 3):
            statistics(0, b)
        aggregate(0)
        copy_out_w(2)
        copy_out_w(3)
        quantise_w(2, 4)
        mx_pass(1, 2)
        mx_pass(1, 3)

        inverse_std(0)
        scale_shift_on_scalar(0)
        for b in range(SAMPLES):
            apply_on_scalar(0, b)
            store(0, b)
            mx_pass(2, b)
        for b in range(SAMPLES):
            statistics(1, b)
        aggregate(1)
        inverse_std(1)
        scale_shift_on_scalar(1)
        for b in range(SAMPLES - 1):
            apply_on_scalar(1, b)
            store(1, b)
            mx_pass(3, b)
        for b in range(SAMPLES):
            statistics(2, b)
        aggregate(2)
        inverse_std(2)
        apply_on_scalar(1, 3)
        store(1, 3)
        mx_pass(3, 3)
        statistics(3, 0)
        scale_shift_on_vector(2)
        for b in range(SAMPLES - 1):
            apply_on_scalar(2, b)
            store(2, b)
        for b in (1, 2, 3):
            statistics(3, b)
        aggregate(3)
        inverse_std(3)
        apply_on_scalar(2, 3)
        store(2, 3)
        scale_shift_on_vector(3)
        apply_on_vector(3, 3)
        for b in (0, 1):
            apply_on_scalar(3, b)
            store(3, b)
        store(3, 3)
        apply_on_scalar(3, 2)
        store(3, 2)
